import numpy as np
import ml_dtypes


def mxq(x, axis, fmt="e4m3"):
    dtype, down = {"e4m3": (ml_dtypes.float8_e4m3fn, 7), "e5m2": (ml_dtypes.float8_e5m2, 14)}[fmt]
    v = np.moveaxis(np.asarray(x, np.float32).astype(ml_dtypes.bfloat16).astype(np.float64), axis, -1)
    blocks = v.reshape(v.shape[:-1] + (-1, 32))
    amax = np.abs(blocks).max(-1, keepdims=True)
    byte = np.maximum(np.where(amax > 0, np.frexp(amax)[1] - 1 + 127, 0) - down, 1)
    scale = np.exp2(byte - 127.0)
    codes = (blocks / scale).astype(np.float32).astype(dtype).astype(np.float64)
    return np.moveaxis((codes * scale).reshape(v.shape), -1, axis)


WIDE = False


def mx_kscale(k):
    if not WIDE:
        return np.ones(k)
    levels = np.array([10, -10, 5, -5, 0])
    a = np.random.permutation(np.resize(levels, k // 512 * 4)).reshape(k // 512, 4)
    idx = np.arange(k)
    return np.exp2(a[idx // 512, idx % 128 // 32])


BF16 = ml_dtypes.bfloat16


def bf(x):
    return np.asarray(x, np.float32).astype(BF16)


def f64(x):
    return np.asarray(x).astype(np.float64)


T, B, D_IN, D_H, D_K, D_OUT = 8, 64, 512, 512, 512, 64


def setup_inputs():
    s, t = mx_kscale(D_H), mx_kscale(D_K)
    return {"h1": bf(np.maximum(np.random.standard_normal((T, B, D_H)), 0.0) * s),
            "W2": bf(np.random.standard_normal((T, D_H, D_K)) * 1.4 / np.sqrt(D_H) / s[:, None] * t),
            "b2": bf(np.random.standard_normal((T, D_K)) * 0.2 * t),
            "W3": bf(np.random.standard_normal((T, D_K, D_OUT)) * 1.4 / np.sqrt(D_K) / t[:, None]),
            "b3": bf(np.random.standard_normal((T, D_OUT)) * 0.2)}


def reference(h1, W2, b2, W3, b3):
    h2 = np.maximum((mxq(f64(h1), 2, "e4m3") @ mxq(f64(W2), 1, "e4m3")) + f64(b2)[:, None, :], 0.0)
    out = (mxq(h2, 2, "e4m3") @ mxq(f64(W3), 1, "e4m3")) + f64(b3)[:, None, :]
    return out.mean(axis=0)

@@ -1,0 +1,239 @@
+from contextlib import ExitStack
+
+import concourse.mybir as mybir
+from concourse.masks import make_identity
+
+BF16 = mybir.dt.bfloat16
+F32 = mybir.dt.float32
+I32 = mybir.dt.int32
+U32 = mybir.dt.uint32
+U8 = mybir.dt.uint8
+FP8X4 = mybir.dt.float8_e4m3fn_x4
+
+P = 128
+PACK = 4
+TREES = 8
+BATCH = 64
+D_HID = 512
+D_MID = 512
+D_OUT = 64
+assert D_HID == P * PACK and D_MID == P * PACK
+
+ROW_TILES = TREES * BATCH // P
+PAIR = 2
+BANK_TILES = 2
+
+VECTOR_COLUMNS = 64
+
+FLOPS = 2 * TREES * BATCH * D_HID * D_MID + 2 * TREES * BATCH * D_MID * D_OUT
+
+
+def tile_randomforestmlp_pa_s_kernel(tc, h1, W2, b2, W3, b3, out):
+    nc = tc.nc
+    with ExitStack() as ctx:
+        const = ctx.enter_context(tc.tile_pool(name="const", bufs=1))
+        raw = ctx.enter_context(tc.tile_pool(name="raw", bufs=1))
+        grouped = ctx.enter_context(tc.tile_pool(name="grouped", bufs=1))
+        packed = ctx.enter_context(tc.tile_pool(name="packed", bufs=1))
+        psum_once = ctx.enter_context(tc.psum_pool(name="psum_once", bufs=1))
+        psum_layer1 = ctx.enter_context(tc.psum_pool(name="psum_layer1", bufs=3))
+        ctx.enter_context(tc.manual_schedule())
+
+        w2_raw = raw.tile([P, TREES, PACK, D_MID], BF16)
+        w3_raw = raw.tile([P, TREES, PACK, D_OUT], BF16)
+        h1_rows = raw.tile([P, ROW_TILES * D_HID], BF16)
+        bias_rows = raw.tile([P, D_MID + D_OUT], BF16)
+
+        w2_grouped = grouped.tile([P, TREES, PACK, P, PACK], BF16, align_bytes=64)
+        w3_grouped = grouped.tile([P, TREES, D_OUT, PACK], BF16, align_bytes=64)
+        h1_grouped = grouped.tile([P, ROW_TILES * P * PACK], BF16, align_bytes=64)
+        h2_sum = grouped.tile([P, TREES, BATCH * PACK], F32)
+        h2_grouped = grouped.tile([P, TREES, BATCH * PACK], BF16, align_bytes=64)
+
+        w2_words = packed.tile([P, TREES, D_MID], U32, align_bytes=64)
+        w2_scales = packed.tile([P, TREES, D_MID], U8, align_bytes=64)
+        h1_words = packed.tile([P, TREES * BATCH], U32, align_bytes=64)
+        h1_scales = packed.tile([P, TREES * BATCH], U8, align_bytes=64)
+        h2_words = packed.tile([P, TREES, P], U32, align_bytes=64)
+        h2_scales = packed.tile([P, TREES, P], U8, align_bytes=64)
+        w3_words = packed.tile([P, (TREES + 1) * D_OUT], U32, align_bytes=64)
+        w3_scales = packed.tile([P, (TREES + 1) * D_OUT], U8, align_bytes=64)
+
+        identity = const.tile([P, P], F32)
+        eighth = const.tile([P, P], BF16)
+        table_warmer = const.tile([P, 1], BF16)
+        b2_columns = const.tile([P, TREES, PACK], F32)
+        b3_mean = const.tile([P, D_OUT], F32)
+        out_rows = const.tile([BATCH, D_OUT], F32)
+
+        nc.vector.memset(bias_rows[:], 0.0)
+        nc.scalar.dma_start(out=bias_rows[0:TREES, 0:D_MID], in_=b2)
+        nc.scalar.dma_start(out=bias_rows[0:TREES, D_MID:], in_=b3)
+
+        def load_w2(t):
+            nc.sync.dma_start(out=w2_raw[:, t], in_=W2[t].rearrange("(p j) n -> p j n", j=PACK))
+
+        load_w2(0)
+        nc.sync.dma_start(
+            out=h1_rows[:].rearrange("p (r k) -> p r k", r=ROW_TILES),
+            in_=h1.rearrange("(r t) b k -> (t b) r k", r=ROW_TILES),
+        )
+        for t in range(1, TREES):
+            load_w2(t)
+        nc.sync.dma_start(out=w3_raw[:], in_=W3.rearrange("t (p j) o -> p t j o", j=PACK))
+
+        make_identity(nc, identity[:])
+        nc.vector.memset(eighth[:], 1.0 / TREES)
+        nc.scalar.activation(out=table_warmer[:], in_=eighth[:, 0:1], func=mybir.ActivationFunctionType.Relu)
+        nc.vector.memset(h2_words[:].bitcast(I32), 0)
+        nc.vector.memset(h2_scales[:].bitcast(I32), 0)
+        nc.vector.memset(w3_words[:, TREES * D_OUT :].bitcast(I32), 0)
+        nc.vector.memset(w3_scales[:, TREES * D_OUT :].bitcast(I32), 0)
+
+        def prepare_biases():
+            b2_pairs = bias_rows[:].bitcast(F32)[:, 0 : D_MID // PAIR].rearrange("p (c u) -> p u c", u=PAIR)
+            b2_psum = psum_once.tile([P, PAIR * P], F32)
+            for u in range(PAIR):
+                nc.tensor.transpose(b2_psum[:, u * P : (u + 1) * P], b2_pairs[:, u, :], identity[:])
+            nc.vector.tensor_copy(
+                out=b2_columns[:].rearrange("p t (u e) -> p t u e", u=PAIR),
+                in_=b2_psum[:].bitcast(BF16).rearrange("p (u row e) -> p row u e", u=PAIR, e=PAIR)[:, 0:TREES],
+            )
+            b3_psum = psum_once.tile([P, D_OUT], F32)
+            nc.tensor.matmul(out=b3_psum[:], lhsT=eighth[:], rhs=bias_rows[:, D_MID:], start=True, stop=True)
+            nc.vector.tensor_copy(out=b3_mean[:], in_=b3_psum[:])
+
+        def prepare_h1():
+            h1_pairs = h1_rows[:].bitcast(F32).rearrange("p (r m u) -> p r u m", r=ROW_TILES, u=PAIR)
+            h1_grouped_pairs = h1_grouped[:].bitcast(F32).rearrange("p (r row u) -> p r row u", r=ROW_TILES, u=PAIR)
+            banks = ROW_TILES // BANK_TILES
+            for bank in range(banks):
+                first = bank * BANK_TILES
+                h1_psum = psum_once.tile([P, BANK_TILES, PAIR, P], F32, name="h1_psum%d" % bank)
+                for r in range(BANK_TILES):
+                    for u in range(PAIR):
+                        nc.tensor.transpose(h1_psum[:, r, u, :], h1_pairs[:, first + r, u, :], identity[:])
+                copy = nc.vector.tensor_copy if bank % 2 == 0 else nc.scalar.copy
+                copy(
+                    out=h1_grouped_pairs[:, first : first + BANK_TILES],
+                    in_=h1_psum[:].rearrange("p r u row -> p r row u"),
+                )
+            bank_rows = BANK_TILES * P
+            for bank in range(banks):
+                nc.vector.quantize_mx(
+                    out=h1_words[:, bank * bank_rows : (bank + 1) * bank_rows].bitcast(FP8X4),
+                    scales=h1_scales[:, bank * bank_rows : (bank + 1) * bank_rows],
+                    in_=h1_grouped[:, bank * bank_rows * PACK : (bank + 1) * bank_rows * PACK],
+                )
+
+        def regroup_w2(t):
+            for copy, columns in (
+                (nc.vector.tensor_copy, slice(0, VECTOR_COLUMNS)),
+                (nc.scalar.copy, slice(VECTOR_COLUMNS, P)),
+            ):
+                copy(
+                    out=w2_grouped[:, t, :, columns, :].rearrange("p i c j -> p c j i"),
+                    in_=w2_raw[:, t].rearrange("p j (c i) -> p c j i", i=PACK)[:, columns],
+                )
+
+        def quantise_w2(t):
+            nc.vector.quantize_mx(
+                out=w2_words[:, t].bitcast(FP8X4),
+                scales=w2_scales[:, t],
+                in_=w2_grouped[:, t].rearrange("p i c j -> p (i c j)"),
+            )
+
+        def regroup_w3():
+            for copy, trees in (
+                (nc.vector.tensor_copy, slice(0, TREES // 2)),
+                (nc.scalar.copy, slice(TREES // 2, TREES)),
+            ):
+                copy(out=w3_grouped[:, trees], in_=w3_raw[:, trees].rearrange("p t j o -> p t o j"))
+
+        def quantise_w3():
+            nc.vector.quantize_mx(
+                out=w3_words[:, 0 : TREES * D_OUT].bitcast(FP8X4),
+                scales=w3_scales[:, 0 : TREES * D_OUT],
+                in_=w3_grouped[:].rearrange("p t o j -> p (t o j)"),
+            )
+
+        layer1_psum = {}
+
+        def layer1(t):
+            layer1_psum[t] = psum_layer1.tile([P, PACK, BATCH], F32, name="layer1_psum")
+            rows = slice(t * BATCH, (t + 1) * BATCH)
+            for i in range(PACK):
+                columns = slice(i * P, (i + 1) * P)
+                nc.tensor.matmul_mx(
+                    out=layer1_psum[t][:, i, :],
+                    lhsT=w2_words[:, t, columns].bitcast(FP8X4),
+                    lhsT_scale=w2_scales[:, t, columns],
+                    rhs=h1_words[:, rows].bitcast(FP8X4),
+                    rhs_scale=h1_scales[:, rows],
+                    start=True,
+                    stop=True,
+                )
+
+        def add_bias(t):
+            nc.vector.tensor_tensor(
+                out=h2_sum[:, t].rearrange("p (b i) -> p b i", i=PACK),
+                in0=layer1_psum[t][:].rearrange("p i b -> p b i"),
+                in1=b2_columns[:, t].unsqueeze(1).to_broadcast([P, BATCH, PACK]),
+                op=mybir.AluOpType.add,
+            )
+
+        def relu(t):
+            nc.scalar.activation(out=h2_grouped[:, t], in_=h2_sum[:, t], func=mybir.ActivationFunctionType.Relu)
+
+        def quantise_h2(t):
+            nc.vector.quantize_mx(
+                out=h2_words[:, t, 0:BATCH].bitcast(FP8X4),
+                scales=h2_scales[:, t, 0:BATCH],
+                in_=h2_grouped[:, t],
+            )
+
+        def is_tree(t):
+            return 0 <= t < TREES
+
+        for step in range(TREES + 3):
+            if is_tree(step - 2):
+                layer1(step - 2)
+            if is_tree(step - 3):
+                relu(step - 3)
+            if is_tree(step - 1):
+                quantise_w2(step - 1)
+            if step - 1 == TREES:
+                quantise_w3()
+            if step == 1:
+                prepare_biases()
+                prepare_h1()
+            if is_tree(step):
+                regroup_w2(step)
+            if step == TREES:
+                regroup_w3()
+            if is_tree(step - 2):
+                add_bias(step - 2)
+            if is_tree(step - 3):
+                quantise_h2(step - 3)
+
+        layer2_psum = psum_once.tile([P, P], F32)
+        for t in range(TREES):
+            columns = slice(t * D_OUT, t * D_OUT + P)
+            nc.tensor.matmul_mx(
+                out=layer2_psum[:],
+                lhsT=h2_words[:, t].bitcast(FP8X4),
+                lhsT_scale=h2_scales[:, t],
+                rhs=w3_words[:, columns].bitcast(FP8X4),
+                rhs_scale=w3_scales[:, columns],
+                start=(t == 0),
+                stop=(t == TREES - 1),
+            )
+        nc.vector.scalar_tensor_tensor(
+            out=out_rows[:],
+            in0=layer2_psum[0:BATCH, 0:D_OUT],
+            scalar=1.0 / TREES,
+            in1=b3_mean[0:BATCH, :],
+            op0=mybir.AluOpType.mult,
+            op1=mybir.AluOpType.add,
+        )
+        nc.sync.dma_start(out=out, in_=out_rows[:])

@@ -35,43 +35,48 @@ def tile_randomforestmlp_pa_s_kernel(tc, h1, W2, b2, W3, b3, out):
         raw = ctx.enter_context(tc.tile_pool(name="raw", bufs=1))
         grouped = ctx.enter_context(tc.tile_pool(name="grouped", bufs=1))
         packed = ctx.enter_context(tc.tile_pool(name="packed", bufs=1))
+        per_tree = ctx.enter_context(tc.tile_pool(name="per_tree", bufs=TREES))
         psum_once = ctx.enter_context(tc.psum_pool(name="psum_once", bufs=1))
         psum_layer1 = ctx.enter_context(tc.psum_pool(name="psum_layer1", bufs=3))
-        ctx.enter_context(tc.manual_schedule())
 
-        w2_raw = raw.tile([P, TREES, PACK, D_MID], BF16)
+        w2_raw = [per_tree.tile([P, PACK, D_MID], BF16, name="w2_raw") for t in range(TREES)]
         w3_raw = raw.tile([P, TREES, PACK, D_OUT], BF16)
         h1_rows = raw.tile([P, ROW_TILES * D_HID], BF16)
-        bias_rows = raw.tile([P, D_MID + D_OUT], BF16)
+        b2_columns = raw.tile([P, TREES, PACK], BF16)
+        b3_rows = raw.tile([P, D_OUT], BF16)
 
-        w2_grouped = grouped.tile([P, TREES, PACK, P, PACK], BF16, align_bytes=64)
+        w2_grouped = [
+            per_tree.tile([P, PACK, P, PACK], BF16, align_bytes=64, name="w2_grouped") for t in range(TREES)
+        ]
         w3_grouped = grouped.tile([P, TREES, D_OUT, PACK], BF16, align_bytes=64)
         h1_grouped = grouped.tile([P, ROW_TILES * P * PACK], BF16, align_bytes=64)
-        h2_sum = grouped.tile([P, TREES, BATCH * PACK], F32)
-        h2_grouped = grouped.tile([P, TREES, BATCH * PACK], BF16, align_bytes=64)
+        h2_sum = [per_tree.tile([P, BATCH * PACK], F32, name="h2_sum") for t in range(TREES)]
+        h2_grouped = [
+            per_tree.tile([P, BATCH * PACK], BF16, align_bytes=64, name="h2_grouped") for t in range(TREES)
+        ]
 
-        w2_words = packed.tile([P, TREES, D_MID], U32, align_bytes=64)
-        w2_scales = packed.tile([P, TREES, D_MID], U8, align_bytes=64)
+        w2_words = [per_tree.tile([P, D_MID], U32, align_bytes=64, name="w2_words") for t in range(TREES)]
+        w2_scales = [per_tree.tile([P, D_MID], U8, align_bytes=64, name="w2_scales") for t in range(TREES)]
         h1_words = packed.tile([P, TREES * BATCH], U32, align_bytes=64)
         h1_scales = packed.tile([P, TREES * BATCH], U8, align_bytes=64)
-        h2_words = packed.tile([P, TREES, P], U32, align_bytes=64)
-        h2_scales = packed.tile([P, TREES, P], U8, align_bytes=64)
+        h2_words = packed.tile([P, (TREES + 1) * BATCH], U32, align_bytes=64)
+        h2_scales = packed.tile([P, (TREES + 1) * BATCH], U8, align_bytes=64)
         w3_words = packed.tile([P, (TREES + 1) * D_OUT], U32, align_bytes=64)
         w3_scales = packed.tile([P, (TREES + 1) * D_OUT], U8, align_bytes=64)
 
         identity = const.tile([P, P], F32)
         eighth = const.tile([P, P], BF16)
         table_warmer = const.tile([P, 1], BF16)
-        b2_columns = const.tile([P, TREES, PACK], F32)
         b3_mean = const.tile([P, D_OUT], F32)
         out_rows = const.tile([BATCH, D_OUT], F32)
 
-        nc.vector.memset(bias_rows[:], 0.0)
-        nc.scalar.dma_start(out=bias_rows[0:TREES, 0:D_MID], in_=b2)
-        nc.scalar.dma_start(out=bias_rows[0:TREES, D_MID:], in_=b3)
+        with nc.allow_non_contiguous_dma(reason="b2 in pieces of 4 values"):
+            nc.scalar.dma_start(out=b2_columns[:], in_=b2.rearrange("t (c i) -> c t i", i=PACK))
+        nc.vector.memset(b3_rows[:], 0.0)
+        nc.scalar.dma_start(out=b3_rows[0:TREES, :], in_=b3)
 
         def load_w2(t):
-            nc.sync.dma_start(out=w2_raw[:, t], in_=W2[t].rearrange("(p j) n -> p j n", j=PACK))
+            nc.sync.dma_start(out=w2_raw[t][:], in_=W2[t].rearrange("(p j) n -> p j n", j=PACK))
 
         load_w2(0)
         nc.sync.dma_start(
@@ -85,23 +90,15 @@ def tile_randomforestmlp_pa_s_kernel(tc, h1, W2, b2, W3, b3, out):
         make_identity(nc, identity[:])
         nc.vector.memset(eighth[:], 1.0 / TREES)
         nc.scalar.activation(out=table_warmer[:], in_=eighth[:, 0:1], func=mybir.ActivationFunctionType.Relu)
-        nc.vector.memset(h2_words[:].bitcast(I32), 0)
-        nc.vector.memset(h2_scales[:].bitcast(I32), 0)
+        nc.vector.memset(h2_words[:, TREES * BATCH :].bitcast(I32), 0)
+        nc.vector.memset(h2_scales[:, TREES * BATCH :].bitcast(I32), 0)
         nc.vector.memset(w3_words[:, TREES * D_OUT :].bitcast(I32), 0)
         nc.vector.memset(w3_scales[:, TREES * D_OUT :].bitcast(I32), 0)
 
-        def prepare_biases():
-            b2_pairs = bias_rows[:].bitcast(F32)[:, 0 : D_MID // PAIR].rearrange("p (c u) -> p u c", u=PAIR)
-            b2_psum = psum_once.tile([P, PAIR * P], F32)
-            for u in range(PAIR):
-                nc.tensor.transpose(b2_psum[:, u * P : (u + 1) * P], b2_pairs[:, u, :], identity[:])
-            nc.vector.tensor_copy(
-                out=b2_columns[:].rearrange("p t (u e) -> p t u e", u=PAIR),
-                in_=b2_psum[:].bitcast(BF16).rearrange("p (u row e) -> p row u e", u=PAIR, e=PAIR)[:, 0:TREES],
-            )
+        def average_b3():
             b3_psum = psum_once.tile([P, D_OUT], F32)
-            nc.tensor.matmul(out=b3_psum[:], lhsT=eighth[:], rhs=bias_rows[:, D_MID:], start=True, stop=True)
-            nc.vector.tensor_copy(out=b3_mean[:], in_=b3_psum[:])
+            nc.tensor.matmul(out=b3_psum[:], lhsT=eighth[:], rhs=b3_rows[:], start=True, stop=True)
+            nc.scalar.copy(out=b3_mean[:], in_=b3_psum[:])
 
         def prepare_h1():
             h1_pairs = h1_rows[:].bitcast(F32).rearrange("p (r m u) -> p r u m", r=ROW_TILES, u=PAIR)
@@ -132,15 +129,15 @@ def tile_randomforestmlp_pa_s_kernel(tc, h1, W2, b2, W3, b3, out):
                 (nc.scalar.copy, slice(VECTOR_COLUMNS, P)),
             ):
                 copy(
-                    out=w2_grouped[:, t, :, columns, :].rearrange("p i c j -> p c j i"),
-                    in_=w2_raw[:, t].rearrange("p j (c i) -> p c j i", i=PACK)[:, columns],
+                    out=w2_grouped[t][:, :, columns, :].rearrange("p i c j -> p c j i"),
+                    in_=w2_raw[t][:].rearrange("p j (c i) -> p c j i", i=PACK)[:, columns],
                 )
 
         def quantise_w2(t):
             nc.vector.quantize_mx(
-                out=w2_words[:, t].bitcast(FP8X4),
-                scales=w2_scales[:, t],
-                in_=w2_grouped[:, t].rearrange("p i c j -> p (i c j)"),
+                out=w2_words[t][:].bitcast(FP8X4),
+                scales=w2_scales[t][:],
+                in_=w2_grouped[t][:].rearrange("p i c j -> p (i c j)"),
             )
 
         def regroup_w3():
@@ -166,8 +163,8 @@ def tile_randomforestmlp_pa_s_kernel(tc, h1, W2, b2, W3, b3, out):
                 columns = slice(i * P, (i + 1) * P)
                 nc.tensor.matmul_mx(
                     out=layer1_psum[t][:, i, :],
-                    lhsT=w2_words[:, t, columns].bitcast(FP8X4),
-                    lhsT_scale=w2_scales[:, t, columns],
+                    lhsT=w2_words[t][:, columns].bitcast(FP8X4),
+                    lhsT_scale=w2_scales[t][:, columns],
                     rhs=h1_words[:, rows].bitcast(FP8X4),
                     rhs_scale=h1_scales[:, rows],
                     start=True,
@@ -176,53 +173,54 @@ def tile_randomforestmlp_pa_s_kernel(tc, h1, W2, b2, W3, b3, out):
 
         def add_bias(t):
             nc.vector.tensor_tensor(
-                out=h2_sum[:, t].rearrange("p (b i) -> p b i", i=PACK),
+                out=h2_sum[t][:].rearrange("p (b i) -> p b i", i=PACK),
                 in0=layer1_psum[t][:].rearrange("p i b -> p b i"),
                 in1=b2_columns[:, t].unsqueeze(1).to_broadcast([P, BATCH, PACK]),
                 op=mybir.AluOpType.add,
             )
 
         def relu(t):
-            nc.scalar.activation(out=h2_grouped[:, t], in_=h2_sum[:, t], func=mybir.ActivationFunctionType.Relu)
+            nc.scalar.activation(out=h2_grouped[t][:], in_=h2_sum[t][:], func=mybir.ActivationFunctionType.Relu)
 
         def quantise_h2(t):
             nc.vector.quantize_mx(
-                out=h2_words[:, t, 0:BATCH].bitcast(FP8X4),
-                scales=h2_scales[:, t, 0:BATCH],
-                in_=h2_grouped[:, t],
+                out=h2_words[:, t * BATCH : (t + 1) * BATCH].bitcast(FP8X4),
+                scales=h2_scales[:, t * BATCH : (t + 1) * BATCH],
+                in_=h2_grouped[t][:],
             )
 
         def is_tree(t):
             return 0 <= t < TREES
 
-        for step in range(TREES + 3):
+        for step in range(TREES + 4):
             if is_tree(step - 2):
                 layer1(step - 2)
-            if is_tree(step - 3):
-                relu(step - 3)
             if is_tree(step - 1):
                 quantise_w2(step - 1)
             if step - 1 == TREES:
                 quantise_w3()
             if step == 1:
-                prepare_biases()
                 prepare_h1()
             if is_tree(step):
                 regroup_w2(step)
             if step == TREES:
                 regroup_w3()
+                average_b3()
             if is_tree(step - 2):
                 add_bias(step - 2)
             if is_tree(step - 3):
-                quantise_h2(step - 3)
+                relu(step - 3)
+            if is_tree(step - 4):
+                quantise_h2(step - 4)
 
         layer2_psum = psum_once.tile([P, P], F32)
         for t in range(TREES):
+            rows = slice(t * BATCH, t * BATCH + P)
             columns = slice(t * D_OUT, t * D_OUT + P)
             nc.tensor.matmul_mx(
                 out=layer2_psum[:],
-                lhsT=h2_words[:, t].bitcast(FP8X4),
-                lhsT_scale=h2_scales[:, t],
+                lhsT=h2_words[:, rows].bitcast(FP8X4),
+                lhsT_scale=h2_scales[:, rows],
                 rhs=w3_words[:, columns].bitcast(FP8X4),
                 rhs_scale=w3_scales[:, columns],
                 start=(t == 0),

@@ -25,6 +25,9 @@ BANK_TILES = 2
 
 VECTOR_COLUMNS = 64
 
+TREES_AHEAD_OF_H1 = 3
+LAYER1_LAG = TREES_AHEAD_OF_H1 + 1
+
 FLOPS = 2 * TREES * BATCH * D_HID * D_MID + 2 * TREES * BATCH * D_MID * D_OUT
 
 
@@ -38,6 +41,7 @@ def tile_randomforestmlp_pa_s_kernel(tc, h1, W2, b2, W3, b3, out):
         per_tree = ctx.enter_context(tc.tile_pool(name="per_tree", bufs=TREES))
         psum_once = ctx.enter_context(tc.psum_pool(name="psum_once", bufs=1))
         psum_layer1 = ctx.enter_context(tc.psum_pool(name="psum_layer1", bufs=3))
+        ctx.enter_context(tc.manual_schedule())
 
         w2_raw = [per_tree.tile([P, PACK, D_MID], BF16, name="w2_raw") for t in range(TREES)]
         w3_raw = raw.tile([P, TREES, PACK, D_OUT], BF16)
@@ -49,7 +53,7 @@ def tile_randomforestmlp_pa_s_kernel(tc, h1, W2, b2, W3, b3, out):
             per_tree.tile([P, PACK, P, PACK], BF16, align_bytes=64, name="w2_grouped") for t in range(TREES)
         ]
         w3_grouped = grouped.tile([P, TREES, D_OUT, PACK], BF16, align_bytes=64)
-        h1_grouped = grouped.tile([P, ROW_TILES * P * PACK], BF16, align_bytes=64)
+        h1_grouped = grouped.tile([P, TREES * BATCH * PACK], BF16, align_bytes=64)
         h2_sum = [per_tree.tile([P, BATCH * PACK], F32, name="h2_sum") for t in range(TREES)]
         h2_grouped = [
             per_tree.tile([P, BATCH * PACK], BF16, align_bytes=64, name="h2_grouped") for t in range(TREES)
@@ -78,12 +82,13 @@ def tile_randomforestmlp_pa_s_kernel(tc, h1, W2, b2, W3, b3, out):
         def load_w2(t):
             nc.sync.dma_start(out=w2_raw[t][:], in_=W2[t].rearrange("(p j) n -> p j n", j=PACK))
 
-        load_w2(0)
+        for t in range(TREES_AHEAD_OF_H1):
+            load_w2(t)
         nc.sync.dma_start(
-            out=h1_rows[:].rearrange("p (r k) -> p r k", r=ROW_TILES),
-            in_=h1.rearrange("(r t) b k -> (t b) r k", r=ROW_TILES),
+            out=h1_rows[:],
+            in_=h1.rearrange("t b k -> (t b) k").rearrange("(q r) k -> q (r k)", r=ROW_TILES),
         )
-        for t in range(1, TREES):
+        for t in range(TREES_AHEAD_OF_H1, TREES):
             load_w2(t)
         nc.sync.dma_start(out=w3_raw[:], in_=W3.rearrange("t (p j) o -> p t j o", j=PACK))
 
@@ -101,27 +106,19 @@ def tile_randomforestmlp_pa_s_kernel(tc, h1, W2, b2, W3, b3, out):
             nc.scalar.copy(out=b3_mean[:], in_=b3_psum[:])
 
         def prepare_h1():
-            h1_pairs = h1_rows[:].bitcast(F32).rearrange("p (r m u) -> p r u m", r=ROW_TILES, u=PAIR)
-            h1_grouped_pairs = h1_grouped[:].bitcast(F32).rearrange("p (r row u) -> p r row u", r=ROW_TILES, u=PAIR)
-            banks = ROW_TILES // BANK_TILES
-            for bank in range(banks):
+            h1_pairs = h1_rows[:].bitcast(F32).rearrange("q (r p u) -> q r u p", r=ROW_TILES, u=PAIR)
+            h1_grouped_pairs = h1_grouped[:].bitcast(F32).rearrange("p (q r u) -> p q r u", r=ROW_TILES, u=PAIR)
+            for bank in range(ROW_TILES // BANK_TILES):
                 first = bank * BANK_TILES
                 h1_psum = psum_once.tile([P, BANK_TILES, PAIR, P], F32, name="h1_psum%d" % bank)
                 for r in range(BANK_TILES):
                     for u in range(PAIR):
                         nc.tensor.transpose(h1_psum[:, r, u, :], h1_pairs[:, first + r, u, :], identity[:])
-                copy = nc.vector.tensor_copy if bank % 2 == 0 else nc.scalar.copy
-                copy(
-                    out=h1_grouped_pairs[:, first : first + BANK_TILES],
-                    in_=h1_psum[:].rearrange("p r u row -> p r row u"),
+                nc.scalar.copy(
+                    out=h1_grouped_pairs[:, :, first : first + BANK_TILES, :],
+                    in_=h1_psum[:].rearrange("p r u q -> p q r u"),
                 )
-            bank_rows = BANK_TILES * P
-            for bank in range(banks):
-                nc.vector.quantize_mx(
-                    out=h1_words[:, bank * bank_rows : (bank + 1) * bank_rows].bitcast(FP8X4),
-                    scales=h1_scales[:, bank * bank_rows : (bank + 1) * bank_rows],
-                    in_=h1_grouped[:, bank * bank_rows * PACK : (bank + 1) * bank_rows * PACK],
-                )
+            nc.vector.quantize_mx(out=h1_words[:].bitcast(FP8X4), scales=h1_scales[:], in_=h1_grouped[:])
 
         def regroup_w2(t):
             for copy, columns in (
@@ -192,26 +189,26 @@ def tile_randomforestmlp_pa_s_kernel(tc, h1, W2, b2, W3, b3, out):
         def is_tree(t):
             return 0 <= t < TREES
 
-        for step in range(TREES + 4):
-            if is_tree(step - 2):
-                layer1(step - 2)
+        for step in range(TREES + LAYER1_LAG + 3):
+            if is_tree(step - LAYER1_LAG):
+                layer1(step - LAYER1_LAG)
             if is_tree(step - 1):
                 quantise_w2(step - 1)
             if step - 1 == TREES:
                 quantise_w3()
-            if step == 1:
+            if step == TREES_AHEAD_OF_H1:
                 prepare_h1()
             if is_tree(step):
                 regroup_w2(step)
             if step == TREES:
                 regroup_w3()
                 average_b3()
-            if is_tree(step - 2):
-                add_bias(step - 2)
-            if is_tree(step - 3):
-                relu(step - 3)
-            if is_tree(step - 4):
-                quantise_h2(step - 4)
+            if is_tree(step - LAYER1_LAG):
+                add_bias(step - LAYER1_LAG)
+            if is_tree(step - LAYER1_LAG - 1):
+                relu(step - LAYER1_LAG - 1)
+            if is_tree(step - LAYER1_LAG - 2):
+                quantise_h2(step - LAYER1_LAG - 2)
 
         layer2_psum = psum_once.tile([P, P], F32)
         for t in range(TREES):

@@ -23,10 +23,10 @@ ROW_TILES = TREES * BATCH // P
 PAIR = 2
 BANK_TILES = 2
 
-VECTOR_COLUMNS = 64
+VECTOR_COLUMNS_FIRST = 80
+VECTOR_COLUMNS = 48
 
-TREES_AHEAD_OF_H1 = 3
-LAYER1_LAG = TREES_AHEAD_OF_H1 + 1
+GROUPS = ((0, 1), (2, 3), (4, 5), (6,), (7,))
 
 FLOPS = 2 * TREES * BATCH * D_HID * D_MID + 2 * TREES * BATCH * D_MID * D_OUT
 
@@ -40,12 +40,12 @@ def tile_randomforestmlp_pa_s_kernel(tc, h1, W2, b2, W3, b3, out):
         packed = ctx.enter_context(tc.tile_pool(name="packed", bufs=1))
         per_tree = ctx.enter_context(tc.tile_pool(name="per_tree", bufs=TREES))
         psum_once = ctx.enter_context(tc.psum_pool(name="psum_once", bufs=1))
-        psum_layer1 = ctx.enter_context(tc.psum_pool(name="psum_layer1", bufs=3))
+        psum_layer1 = ctx.enter_context(tc.psum_pool(name="psum_layer1", bufs=4))
         ctx.enter_context(tc.manual_schedule())
 
         w2_raw = [per_tree.tile([P, PACK, D_MID], BF16, name="w2_raw") for t in range(TREES)]
         w3_raw = raw.tile([P, TREES, PACK, D_OUT], BF16)
-        h1_rows = raw.tile([P, ROW_TILES * D_HID], BF16)
+        h1_rows = raw.tile([P, ROW_TILES, D_HID], BF16)
         b2_columns = raw.tile([P, TREES, PACK], BF16)
         b3_rows = raw.tile([P, D_OUT], BF16)
 
@@ -54,9 +54,11 @@ def tile_randomforestmlp_pa_s_kernel(tc, h1, W2, b2, W3, b3, out):
         ]
         w3_grouped = grouped.tile([P, TREES, D_OUT, PACK], BF16, align_bytes=64)
         h1_grouped = grouped.tile([P, TREES * BATCH * PACK], BF16, align_bytes=64)
-        h2_sum = [per_tree.tile([P, BATCH * PACK], F32, name="h2_sum") for t in range(TREES)]
+        h2_sum = [
+            per_tree.tile([P, len(g) * BATCH * PACK], F32, name="h2_sum") for g in GROUPS
+        ]
         h2_grouped = [
-            per_tree.tile([P, BATCH * PACK], BF16, align_bytes=64, name="h2_grouped") for t in range(TREES)
+            per_tree.tile([P, len(g) * BATCH * PACK], BF16, align_bytes=64, name="h2_grouped") for g in GROUPS
         ]
 
         w2_words = [per_tree.tile([P, D_MID], U32, align_bytes=64, name="w2_words") for t in range(TREES)]
@@ -74,21 +76,20 @@ def tile_randomforestmlp_pa_s_kernel(tc, h1, W2, b2, W3, b3, out):
         b3_mean = const.tile([P, D_OUT], F32)
         out_rows = const.tile([BATCH, D_OUT], F32)
 
-        with nc.allow_non_contiguous_dma(reason="b2 in pieces of 4 values"):
-            nc.scalar.dma_start(out=b2_columns[:], in_=b2.rearrange("t (c i) -> c t i", i=PACK))
-        nc.vector.memset(b3_rows[:], 0.0)
-        nc.scalar.dma_start(out=b3_rows[0:TREES, :], in_=b3)
-
         def load_w2(t):
             nc.sync.dma_start(out=w2_raw[t][:], in_=W2[t].rearrange("(p j) n -> p j n", j=PACK))
 
-        for t in range(TREES_AHEAD_OF_H1):
-            load_w2(t)
-        nc.sync.dma_start(
-            out=h1_rows[:],
-            in_=h1.rearrange("t b k -> (t b) k").rearrange("(q r) k -> q (r k)", r=ROW_TILES),
-        )
-        for t in range(TREES_AHEAD_OF_H1, TREES):
+        h1_tiles = h1.rearrange("t b k -> (t b) k").rearrange("(r q) k -> q r k", q=P)
+        for bank in range(ROW_TILES // BANK_TILES):
+            tiles = slice(bank * BANK_TILES, (bank + 1) * BANK_TILES)
+            nc.sync.dma_start(out=h1_rows[:, tiles, :], in_=h1_tiles[:, tiles, :])
+        load_w2(0)
+        load_w2(1)
+        with nc.allow_non_contiguous_dma(reason="b2 in pieces of 4 values"):
+            nc.sync.dma_start(out=b2_columns[:], in_=b2.rearrange("t (c i) -> c t i", i=PACK))
+        nc.vector.memset(b3_rows[:], 0.0)
+        nc.sync.dma_start(out=b3_rows[0:TREES, :], in_=b3)
+        for t in range(2, TREES):
             load_w2(t)
         nc.sync.dma_start(out=w3_raw[:], in_=W3.rearrange("t (p j) o -> p t j o", j=PACK))
 
@@ -105,25 +106,37 @@ def tile_randomforestmlp_pa_s_kernel(tc, h1, W2, b2, W3, b3, out):
             nc.tensor.matmul(out=b3_psum[:], lhsT=eighth[:], rhs=b3_rows[:], start=True, stop=True)
             nc.scalar.copy(out=b3_mean[:], in_=b3_psum[:])
 
-        def prepare_h1():
-            h1_pairs = h1_rows[:].bitcast(F32).rearrange("q (r p u) -> q r u p", r=ROW_TILES, u=PAIR)
-            h1_grouped_pairs = h1_grouped[:].bitcast(F32).rearrange("p (q r u) -> p q r u", r=ROW_TILES, u=PAIR)
-            for bank in range(ROW_TILES // BANK_TILES):
-                first = bank * BANK_TILES
-                h1_psum = psum_once.tile([P, BANK_TILES, PAIR, P], F32, name="h1_psum%d" % bank)
-                for r in range(BANK_TILES):
-                    for u in range(PAIR):
-                        nc.tensor.transpose(h1_psum[:, r, u, :], h1_pairs[:, first + r, u, :], identity[:])
-                nc.scalar.copy(
-                    out=h1_grouped_pairs[:, :, first : first + BANK_TILES, :],
-                    in_=h1_psum[:].rearrange("p r u q -> p q r u"),
-                )
-            nc.vector.quantize_mx(out=h1_words[:].bitcast(FP8X4), scales=h1_scales[:], in_=h1_grouped[:])
+        h1_pairs = h1_rows[:].rearrange("q r k -> q (r k)").bitcast(F32).rearrange("q (r p u) -> q r u p", r=ROW_TILES, u=PAIR)
+        h1_grouped_pairs = h1_grouped[:].bitcast(F32).rearrange("p (r q u) -> p r q u", r=ROW_TILES, u=PAIR)
+        h1_psum = {}
+
+        def transpose_h1(bank):
+            first = bank * BANK_TILES
+            h1_psum[bank] = psum_once.tile([P, BANK_TILES, PAIR, P], F32, name="h1_psum%d" % bank)
+            for r in range(BANK_TILES):
+                for u in range(PAIR):
+                    nc.tensor.transpose(h1_psum[bank][:, r, u, :], h1_pairs[:, first + r, u, :], identity[:])
+
+        def copy_h1(bank, copy):
+            first = bank * BANK_TILES
+            copy(
+                out=h1_grouped_pairs[:, first : first + BANK_TILES],
+                in_=h1_psum[bank][:].rearrange("p r u q -> p r q u"),
+            )
+
+        def quantise_h1(bank):
+            rows = slice(bank * BANK_TILES * P, (bank + 1) * BANK_TILES * P)
+            nc.vector.quantize_mx(
+                out=h1_words[:, rows].bitcast(FP8X4),
+                scales=h1_scales[:, rows],
+                in_=h1_grouped[:, bank * BANK_TILES * P * PACK : (bank + 1) * BANK_TILES * P * PACK],
+            )
 
         def regroup_w2(t):
+            vector_columns = VECTOR_COLUMNS_FIRST if t == 0 else VECTOR_COLUMNS
             for copy, columns in (
-                (nc.vector.tensor_copy, slice(0, VECTOR_COLUMNS)),
-                (nc.scalar.copy, slice(VECTOR_COLUMNS, P)),
+                (nc.vector.tensor_copy, slice(0, vector_columns)),
+                (nc.scalar.copy, slice(vector_columns, P)),
             ):
                 copy(
                     out=w2_grouped[t][:, :, columns, :].rearrange("p i c j -> p c j i"),
@@ -139,8 +152,8 @@ def tile_randomforestmlp_pa_s_kernel(tc, h1, W2, b2, W3, b3, out):
 
         def regroup_w3():
             for copy, trees in (
-                (nc.vector.tensor_copy, slice(0, TREES // 2)),
-                (nc.scalar.copy, slice(TREES // 2, TREES)),
+                (nc.vector.tensor_copy, slice(0, 3)),
+                (nc.scalar.copy, slice(3, TREES)),
             ):
                 copy(out=w3_grouped[:, trees], in_=w3_raw[:, trees].rearrange("p t j o -> p t o j"))
 
@@ -154,12 +167,14 @@ def tile_randomforestmlp_pa_s_kernel(tc, h1, W2, b2, W3, b3, out):
         layer1_psum = {}
 
         def layer1(t):
-            layer1_psum[t] = psum_layer1.tile([P, PACK, BATCH], F32, name="layer1_psum")
+            g = [n for n in range(len(GROUPS)) if t in GROUPS[n]][0]
+            if t == GROUPS[g][0]:
+                layer1_psum[g] = psum_layer1.tile([P, len(GROUPS[g]), PACK, BATCH], F32, name="layer1_psum")
             rows = slice(t * BATCH, (t + 1) * BATCH)
             for i in range(PACK):
                 columns = slice(i * P, (i + 1) * P)
                 nc.tensor.matmul_mx(
-                    out=layer1_psum[t][:, i, :],
+                    out=layer1_psum[g][:, t - GROUPS[g][0], i, :],
                     lhsT=w2_words[t][:, columns].bitcast(FP8X4),
                     lhsT_scale=w2_scales[t][:, columns],
                     rhs=h1_words[:, rows].bitcast(FP8X4),
@@ -168,47 +183,61 @@ def tile_randomforestmlp_pa_s_kernel(tc, h1, W2, b2, W3, b3, out):
                     stop=True,
                 )
 
-        def add_bias(t):
+        def add_bias(g):
+            trees = GROUPS[g]
             nc.vector.tensor_tensor(
-                out=h2_sum[t][:].rearrange("p (b i) -> p b i", i=PACK),
-                in0=layer1_psum[t][:].rearrange("p i b -> p b i"),
-                in1=b2_columns[:, t].unsqueeze(1).to_broadcast([P, BATCH, PACK]),
+                out=h2_sum[g][:].rearrange("p (t b i) -> p t b i", t=len(trees), i=PACK),
+                in0=layer1_psum[g][:].rearrange("p t i b -> p t b i"),
+                in1=b2_columns[:, trees[0] : trees[0] + len(trees)].unsqueeze(2).to_broadcast([P, len(trees), BATCH, PACK]),
                 op=mybir.AluOpType.add,
             )
 
-        def relu(t):
-            nc.scalar.activation(out=h2_grouped[t][:], in_=h2_sum[t][:], func=mybir.ActivationFunctionType.Relu)
+        def relu(g):
+            nc.scalar.activation(out=h2_grouped[g][:], in_=h2_sum[g][:], func=mybir.ActivationFunctionType.Relu)
 
-        def quantise_h2(t):
+        def quantise_h2(g):
+            rows = slice(GROUPS[g][0] * BATCH, (GROUPS[g][-1] + 1) * BATCH)
             nc.vector.quantize_mx(
-                out=h2_words[:, t * BATCH : (t + 1) * BATCH].bitcast(FP8X4),
-                scales=h2_scales[:, t * BATCH : (t + 1) * BATCH],
-                in_=h2_grouped[t][:],
+                out=h2_words[:, rows].bitcast(FP8X4),
+                scales=h2_scales[:, rows],
+                in_=h2_grouped[g][:],
             )
+
+        for bank in range(ROW_TILES // BANK_TILES):
+            transpose_h1(bank)
+        copy_h1(0, nc.vector.tensor_copy)
+        copy_h1(1, nc.scalar.copy)
 
         def is_tree(t):
             return 0 <= t < TREES
 
-        for step in range(TREES + LAYER1_LAG + 3):
-            if is_tree(step - LAYER1_LAG):
-                layer1(step - LAYER1_LAG)
-            if is_tree(step - 1):
-                quantise_w2(step - 1)
-            if step - 1 == TREES:
-                quantise_w3()
-            if step == TREES_AHEAD_OF_H1:
-                prepare_h1()
+        def bias_step(g):
+            return GROUPS[g][-1] + 2
+
+        for step in range(TREES + 4):
+            if is_tree(step - 2):
+                layer1(step - 2)
             if is_tree(step):
                 regroup_w2(step)
             if step == TREES:
                 regroup_w3()
                 average_b3()
-            if is_tree(step - LAYER1_LAG):
-                add_bias(step - LAYER1_LAG)
-            if is_tree(step - LAYER1_LAG - 1):
-                relu(step - LAYER1_LAG - 1)
-            if is_tree(step - LAYER1_LAG - 2):
-                quantise_h2(step - LAYER1_LAG - 2)
+            if step == 0:
+                quantise_h1(0)
+                quantise_h1(1)
+            if is_tree(step - 1):
+                quantise_w2(step - 1)
+            if step - 1 == TREES:
+                quantise_w3()
+            for g in range(len(GROUPS)):
+                if bias_step(g) == step:
+                    add_bias(g)
+            for g in range(len(GROUPS)):
+                if bias_step(g) + 1 == step:
+                    relu(g)
+            for g in range(len(GROUPS)):
+                if bias_step(g) + 2 == step:
+                    quantise_h2(g)
 
         layer2_psum = psum_once.tile([P, P], F32)
         for t in range(TREES):

@@ -47,6 +47,7 @@ def tile_randomforestmlp_pa_s_kernel(tc, h1, W2, b2, W3, b3, out):
         w3_raw = raw.tile([P, TREES, PACK, D_OUT], BF16)
         h1_rows = raw.tile([P, ROW_TILES, D_HID], BF16)
         b2_columns = raw.tile([P, TREES, PACK], BF16)
+        b2_rows = raw.tile([P, D_MID], BF16)
         b3_rows = raw.tile([P, D_OUT], BF16)
 
         w2_grouped = [
@@ -83,15 +84,14 @@ def tile_randomforestmlp_pa_s_kernel(tc, h1, W2, b2, W3, b3, out):
         for bank in range(ROW_TILES // BANK_TILES):
             tiles = slice(bank * BANK_TILES, (bank + 1) * BANK_TILES)
             nc.sync.dma_start(out=h1_rows[:, tiles, :], in_=h1_tiles[:, tiles, :])
-        load_w2(0)
-        load_w2(1)
-        with nc.allow_non_contiguous_dma(reason="b2 in pieces of 4 values"):
-            nc.sync.dma_start(out=b2_columns[:], in_=b2.rearrange("t (c i) -> c t i", i=PACK))
-        nc.vector.memset(b3_rows[:], 0.0)
-        nc.sync.dma_start(out=b3_rows[0:TREES, :], in_=b3)
-        for t in range(2, TREES):
+        for t in range(TREES):
             load_w2(t)
         nc.sync.dma_start(out=w3_raw[:], in_=W3.rearrange("t (p j) o -> p t j o", j=PACK))
+
+        nc.vector.memset(b2_rows[:], 0.0)
+        nc.vector.memset(b3_rows[:], 0.0)
+        nc.scalar.dma_start(out=b2_rows[0:TREES, :], in_=b2)
+        nc.scalar.dma_start(out=b3_rows[0:TREES, :], in_=b3)
 
         make_identity(nc, identity[:])
         nc.vector.memset(eighth[:], 1.0 / TREES)
@@ -101,10 +101,17 @@ def tile_randomforestmlp_pa_s_kernel(tc, h1, W2, b2, W3, b3, out):
         nc.vector.memset(w3_words[:, TREES * D_OUT :].bitcast(I32), 0)
         nc.vector.memset(w3_scales[:, TREES * D_OUT :].bitcast(I32), 0)
 
-        def average_b3():
-            b3_psum = psum_once.tile([P, D_OUT], F32)
-            nc.tensor.matmul(out=b3_psum[:], lhsT=eighth[:], rhs=b3_rows[:], start=True, stop=True)
-            nc.scalar.copy(out=b3_mean[:], in_=b3_psum[:])
+        def prepare_biases():
+            bias_psum = psum_once.tile([P, PAIR * P + D_OUT], F32)
+            b2_pairs = b2_rows[:].bitcast(F32).rearrange("t (c u) -> t u c", u=PAIR)
+            for u in range(PAIR):
+                nc.tensor.transpose(bias_psum[:, u * P : (u + 1) * P], b2_pairs[:, u, :], identity[:])
+            nc.tensor.matmul(out=bias_psum[:, PAIR * P :], lhsT=eighth[:], rhs=b3_rows[:], start=True, stop=True)
+            nc.scalar.copy(
+                out=b2_columns[:].rearrange("c t i -> c (t i)").bitcast(F32).rearrange("c (t u) -> c t u", u=PAIR),
+                in_=bias_psum[:, 0 : PAIR * P].rearrange("c (u t) -> c t u", u=PAIR)[:, 0:TREES, :],
+            )
+            nc.scalar.copy(out=b3_mean[:], in_=bias_psum[:, PAIR * P :])
 
         h1_pairs = h1_rows[:].rearrange("q r k -> q (r k)").bitcast(F32).rearrange("q (r p u) -> q r u p", r=ROW_TILES, u=PAIR)
         h1_grouped_pairs = h1_grouped[:].bitcast(F32).rearrange("p (r q u) -> p r q u", r=ROW_TILES, u=PAIR)
@@ -152,8 +159,8 @@ def tile_randomforestmlp_pa_s_kernel(tc, h1, W2, b2, W3, b3, out):
 
         def regroup_w3():
             for copy, trees in (
-                (nc.vector.tensor_copy, slice(0, 3)),
-                (nc.scalar.copy, slice(3, TREES)),
+                (nc.vector.tensor_copy, slice(0, TREES // 2)),
+                (nc.scalar.copy, slice(TREES // 2, TREES)),
             ):
                 copy(out=w3_grouped[:, trees], in_=w3_raw[:, trees].rearrange("p t j o -> p t o j"))
 
@@ -221,8 +228,8 @@ def tile_randomforestmlp_pa_s_kernel(tc, h1, W2, b2, W3, b3, out):
                 regroup_w2(step)
             if step == TREES:
                 regroup_w3()
-                average_b3()
             if step == 0:
+                prepare_biases()
                 quantise_h1(0)
                 quantise_h1(1)
             if is_tree(step - 1):

@@ -24,7 +24,7 @@ PAIR = 2
 BANK_TILES = 2
 
 VECTOR_COLUMNS_FIRST = 80
-VECTOR_COLUMNS = 48
+VECTOR_COLUMNS = 60
 
 GROUPS = ((0, 1), (2, 3), (4, 5), (6,), (7,))
 
@@ -80,18 +80,17 @@ def tile_randomforestmlp_pa_s_kernel(tc, h1, W2, b2, W3, b3, out):
         def load_w2(t):
             nc.sync.dma_start(out=w2_raw[t][:], in_=W2[t].rearrange("(p j) n -> p j n", j=PACK))
 
+        nc.vector.memset(b2_rows[:].bitcast(F32), 0.0)
+        nc.vector.memset(b3_rows[:].bitcast(F32), 0.0)
         h1_tiles = h1.rearrange("t b k -> (t b) k").rearrange("(r q) k -> q r k", q=P)
         for bank in range(ROW_TILES // BANK_TILES):
             tiles = slice(bank * BANK_TILES, (bank + 1) * BANK_TILES)
             nc.sync.dma_start(out=h1_rows[:, tiles, :], in_=h1_tiles[:, tiles, :])
+        nc.sync.dma_start(out=b2_rows[0:TREES, :], in_=b2)
+        nc.sync.dma_start(out=b3_rows[0:TREES, :], in_=b3)
         for t in range(TREES):
             load_w2(t)
         nc.sync.dma_start(out=w3_raw[:], in_=W3.rearrange("t (p j) o -> p t j o", j=PACK))
-
-        nc.vector.memset(b2_rows[:], 0.0)
-        nc.vector.memset(b3_rows[:], 0.0)
-        nc.scalar.dma_start(out=b2_rows[0:TREES, :], in_=b2)
-        nc.scalar.dma_start(out=b3_rows[0:TREES, :], in_=b3)
 
         make_identity(nc, identity[:])
         nc.vector.memset(eighth[:], 1.0 / TREES)

@@ -28,6 +28,8 @@ VECTOR_COLUMNS = 60
 
 GROUPS = ((0, 1), (2, 3), (4, 5), (6,), (7,))
 
+LAYER1_LAG = 3
+
 FLOPS = 2 * TREES * BATCH * D_HID * D_MID + 2 * TREES * BATCH * D_MID * D_OUT
 
 
@@ -218,11 +220,11 @@ def tile_randomforestmlp_pa_s_kernel(tc, h1, W2, b2, W3, b3, out):
             return 0 <= t < TREES
 
         def bias_step(g):
-            return GROUPS[g][-1] + 2
+            return GROUPS[g][-1] + LAYER1_LAG
 
-        for step in range(TREES + 4):
-            if is_tree(step - 2):
-                layer1(step - 2)
+        for step in range(TREES + LAYER1_LAG + 2):
+            if is_tree(step - LAYER1_LAG):
+                layer1(step - LAYER1_LAG)
             if is_tree(step):
                 regroup_w2(step)
             if step == TREES:

@@ -58,7 +58,7 @@ def tile_randomforestmlp_pa_s_kernel(tc, h1, W2, b2, W3, b3, out):
         w3_grouped = grouped.tile([P, TREES, D_OUT, PACK], BF16, align_bytes=64)
         h1_grouped = grouped.tile([P, TREES * BATCH * PACK], BF16, align_bytes=64)
         h2_sum = [
-            per_tree.tile([P, len(g) * BATCH * PACK], F32, name="h2_sum") for g in GROUPS
+            per_tree.tile([P, len(g) * BATCH * PACK], F32 if len(g) > 1 else BF16, name="h2_sum") for g in GROUPS
         ]
         h2_grouped = [
             per_tree.tile([P, len(g) * BATCH * PACK], BF16, align_bytes=64, name="h2_grouped") for g in GROUPS
@@ -68,8 +68,8 @@ def tile_randomforestmlp_pa_s_kernel(tc, h1, W2, b2, W3, b3, out):
         w2_scales = [per_tree.tile([P, D_MID], U8, align_bytes=64, name="w2_scales") for t in range(TREES)]
         h1_words = packed.tile([P, TREES * BATCH], U32, align_bytes=64)
         h1_scales = packed.tile([P, TREES * BATCH], U8, align_bytes=64)
-        h2_words = packed.tile([P, (TREES + 1) * BATCH], U32, align_bytes=64)
-        h2_scales = packed.tile([P, (TREES + 1) * BATCH], U8, align_bytes=64)
+        h2_words = packed.tile([P, (TREES + 2) * BATCH], U32, align_bytes=64)
+        h2_scales = packed.tile([P, (TREES + 2) * BATCH], U8, align_bytes=64)
         w3_words = packed.tile([P, (TREES + 1) * D_OUT], U32, align_bytes=64)
         w3_scales = packed.tile([P, (TREES + 1) * D_OUT], U8, align_bytes=64)
 
@@ -97,8 +97,8 @@ def tile_randomforestmlp_pa_s_kernel(tc, h1, W2, b2, W3, b3, out):
         make_identity(nc, identity[:])
         nc.vector.memset(eighth[:], 1.0 / TREES)
         nc.scalar.activation(out=table_warmer[:], in_=eighth[:, 0:1], func=mybir.ActivationFunctionType.Relu)
-        nc.vector.memset(h2_words[:, TREES * BATCH :].bitcast(I32), 0)
-        nc.vector.memset(h2_scales[:, TREES * BATCH :].bitcast(I32), 0)
+        nc.vector.memset(h2_words[:].bitcast(I32), 0)
+        nc.vector.memset(h2_scales[:].bitcast(I32), 0)
         nc.vector.memset(w3_words[:, TREES * D_OUT :].bitcast(I32), 0)
         nc.vector.memset(w3_scales[:, TREES * D_OUT :].bitcast(I32), 0)
 
@@ -201,10 +201,16 @@ def tile_randomforestmlp_pa_s_kernel(tc, h1, W2, b2, W3, b3, out):
             )
 
         def relu(g):
-            nc.scalar.activation(out=h2_grouped[g][:], in_=h2_sum[g][:], func=mybir.ActivationFunctionType.Relu)
+            if len(GROUPS[g]) > 1:
+                nc.scalar.activation(out=h2_grouped[g][:], in_=h2_sum[g][:], func=mybir.ActivationFunctionType.Relu)
+            else:
+                nc.vector.tensor_scalar_max(out=h2_grouped[g][:], in0=h2_sum[g][:], scalar1=0.0)
+
+        def place(t):
+            return t * BATCH if t < TREES - 1 else (t + 1) * BATCH
 
         def quantise_h2(g):
-            rows = slice(GROUPS[g][0] * BATCH, (GROUPS[g][-1] + 1) * BATCH)
+            rows = slice(place(GROUPS[g][0]), place(GROUPS[g][-1]) + BATCH)
             nc.vector.quantize_mx(
                 out=h2_words[:, rows].bitcast(FP8X4),
                 scales=h2_scales[:, rows],
@@ -249,7 +255,7 @@ def tile_randomforestmlp_pa_s_kernel(tc, h1, W2, b2, W3, b3, out):
 
         layer2_psum = psum_once.tile([P, P], F32)
         for t in range(TREES):
-            rows = slice(t * BATCH, t * BATCH + P)
+            rows = slice(place(t), place(t) + P)
             columns = slice(t * D_OUT, t * D_OUT + P)
             nc.tensor.matmul_mx(
                 out=layer2_psum[:],

@@ -68,10 +68,10 @@ def tile_randomforestmlp_pa_s_kernel(tc, h1, W2, b2, W3, b3, out):
         w2_scales = [per_tree.tile([P, D_MID], U8, align_bytes=64, name="w2_scales") for t in range(TREES)]
         h1_words = packed.tile([P, TREES * BATCH], U32, align_bytes=64)
         h1_scales = packed.tile([P, TREES * BATCH], U8, align_bytes=64)
-        h2_words = packed.tile([P, (TREES + 2) * BATCH], U32, align_bytes=64)
-        h2_scales = packed.tile([P, (TREES + 2) * BATCH], U8, align_bytes=64)
-        w3_words = packed.tile([P, (TREES + 1) * D_OUT], U32, align_bytes=64)
-        w3_scales = packed.tile([P, (TREES + 1) * D_OUT], U8, align_bytes=64)
+        h2_words = packed.tile([P, (TREES + len(GROUPS)) * BATCH], U32, align_bytes=64)
+        h2_scales = packed.tile([P, (TREES + len(GROUPS)) * BATCH], U8, align_bytes=64)
+        w3_words = packed.tile([P, (TREES + 2) * D_OUT], U32, align_bytes=64)
+        w3_scales = packed.tile([P, (TREES + 2) * D_OUT], U8, align_bytes=64)
 
         identity = const.tile([P, P], F32)
         eighth = const.tile([P, P], BF16)
@@ -99,8 +99,8 @@ def tile_randomforestmlp_pa_s_kernel(tc, h1, W2, b2, W3, b3, out):
         nc.scalar.activation(out=table_warmer[:], in_=eighth[:, 0:1], func=mybir.ActivationFunctionType.Relu)
         nc.vector.memset(h2_words[:].bitcast(I32), 0)
         nc.vector.memset(h2_scales[:].bitcast(I32), 0)
-        nc.vector.memset(w3_words[:, TREES * D_OUT :].bitcast(I32), 0)
-        nc.vector.memset(w3_scales[:, TREES * D_OUT :].bitcast(I32), 0)
+        nc.vector.memset(w3_words[:].bitcast(I32), 0)
+        nc.vector.memset(w3_scales[:].bitcast(I32), 0)
 
         def prepare_biases():
             bias_psum = psum_once.tile([P, PAIR * P + D_OUT], F32)
@@ -165,11 +165,16 @@ def tile_randomforestmlp_pa_s_kernel(tc, h1, W2, b2, W3, b3, out):
             ):
                 copy(out=w3_grouped[:, trees], in_=w3_raw[:, trees].rearrange("p t j o -> p t o j"))
 
-        def quantise_w3():
+        def place_w3(t):
+            return (t + t // (TREES // 2)) * D_OUT
+
+        def quantise_w3(half):
+            first = half * (TREES // 2)
+            columns = slice(place_w3(first), place_w3(first) + (TREES // 2) * D_OUT)
             nc.vector.quantize_mx(
-                out=w3_words[:, 0 : TREES * D_OUT].bitcast(FP8X4),
-                scales=w3_scales[:, 0 : TREES * D_OUT],
-                in_=w3_grouped[:].rearrange("p t o j -> p (t o j)"),
+                out=w3_words[:, columns].bitcast(FP8X4),
+                scales=w3_scales[:, columns],
+                in_=w3_grouped[:, first : first + TREES // 2].rearrange("p t o j -> p (t o j)"),
             )
 
         layer1_psum = {}
@@ -207,7 +212,7 @@ def tile_randomforestmlp_pa_s_kernel(tc, h1, W2, b2, W3, b3, out):
                 nc.vector.tensor_scalar_max(out=h2_grouped[g][:], in0=h2_sum[g][:], scalar1=0.0)
 
         def place(t):
-            return t * BATCH if t < TREES - 1 else (t + 1) * BATCH
+            return (t + [n for n in range(len(GROUPS)) if t in GROUPS[n]][0]) * BATCH
 
         def quantise_h2(g):
             rows = slice(place(GROUPS[g][0]), place(GROUPS[g][-1]) + BATCH)
@@ -241,8 +246,10 @@ def tile_randomforestmlp_pa_s_kernel(tc, h1, W2, b2, W3, b3, out):
                 quantise_h1(1)
             if is_tree(step - 1):
                 quantise_w2(step - 1)
+            if step == TREES:
+                quantise_w3(0)
             if step - 1 == TREES:
-                quantise_w3()
+                quantise_w3(1)
             for g in range(len(GROUPS)):
                 if bias_step(g) == step:
                     add_bias(g)
@@ -256,7 +263,7 @@ def tile_randomforestmlp_pa_s_kernel(tc, h1, W2, b2, W3, b3, out):
         layer2_psum = psum_once.tile([P, P], F32)
         for t in range(TREES):
             rows = slice(place(t), place(t) + P)
-            columns = slice(t * D_OUT, t * D_OUT + P)
+            columns = slice(place_w3(t), place_w3(t) + P)
             nc.tensor.matmul_mx(
                 out=layer2_psum[:],
                 lhsT=h2_words[:, rows].bitcast(FP8X4),

@@ -225,7 +225,6 @@ def tile_randomforestmlp_pa_s_kernel(tc, h1, W2, b2, W3, b3, out):
         for bank in range(ROW_TILES // BANK_TILES):
             transpose_h1(bank)
         copy_h1(0, nc.vector.tensor_copy)
-        copy_h1(1, nc.scalar.copy)
 
         def is_tree(t):
             return 0 <= t < TREES
@@ -241,11 +240,14 @@ def tile_randomforestmlp_pa_s_kernel(tc, h1, W2, b2, W3, b3, out):
             if step == TREES:
                 regroup_w3()
             if step == 0:
-                prepare_biases()
+                copy_h1(1, nc.scalar.copy)
                 quantise_h1(0)
-                quantise_h1(1)
+            if step == 2:
+                prepare_biases()
             if is_tree(step - 1):
                 quantise_w2(step - 1)
+            if step == 1:
+                quantise_h1(1)
             if step == TREES:
                 quantise_w3(0)
             if step - 1 == TREES:

@@ -84,10 +84,10 @@ def tile_randomforestmlp_pa_s_kernel(tc, h1, W2, b2, W3, b3, out):
 
         nc.vector.memset(b2_rows[:].bitcast(F32), 0.0)
         nc.vector.memset(b3_rows[:].bitcast(F32), 0.0)
-        h1_tiles = h1.rearrange("t b k -> (t b) k").rearrange("(r q) k -> q r k", q=P)
+        h1_tiles = h1.rearrange("t b k -> (t b) k").rearrange("(bank q r) k -> q bank r k", q=P, r=BANK_TILES)
         for bank in range(ROW_TILES // BANK_TILES):
             tiles = slice(bank * BANK_TILES, (bank + 1) * BANK_TILES)
-            nc.sync.dma_start(out=h1_rows[:, tiles, :], in_=h1_tiles[:, tiles, :])
+            nc.sync.dma_start(out=h1_rows[:, tiles, :], in_=h1_tiles[:, bank])
         nc.sync.dma_start(out=b2_rows[0:TREES, :], in_=b2)
         nc.sync.dma_start(out=b3_rows[0:TREES, :], in_=b3)
         for t in range(TREES):
@@ -115,7 +115,7 @@ def tile_randomforestmlp_pa_s_kernel(tc, h1, W2, b2, W3, b3, out):
             nc.scalar.copy(out=b3_mean[:], in_=bias_psum[:, PAIR * P :])
 
         h1_pairs = h1_rows[:].rearrange("q r k -> q (r k)").bitcast(F32).rearrange("q (r p u) -> q r u p", r=ROW_TILES, u=PAIR)
-        h1_grouped_pairs = h1_grouped[:].bitcast(F32).rearrange("p (r q u) -> p r q u", r=ROW_TILES, u=PAIR)
+        h1_grouped_pairs = h1_grouped[:].bitcast(F32).rearrange("p (bank q r u) -> p bank q r u", q=P, r=BANK_TILES, u=PAIR)
         h1_psum = {}
 
         def transpose_h1(bank):
@@ -126,10 +126,9 @@ def tile_randomforestmlp_pa_s_kernel(tc, h1, W2, b2, W3, b3, out):
                     nc.tensor.transpose(h1_psum[bank][:, r, u, :], h1_pairs[:, first + r, u, :], identity[:])
 
         def copy_h1(bank, copy):
-            first = bank * BANK_TILES
             copy(
-                out=h1_grouped_pairs[:, first : first + BANK_TILES],
-                in_=h1_psum[bank][:].rearrange("p r u q -> p r q u"),
+                out=h1_grouped_pairs[:, bank],
+                in_=h1_psum[bank][:].rearrange("p r u q -> p q r u"),
             )
 
         def quantise_h1(bank):
@@ -163,7 +162,10 @@ def tile_randomforestmlp_pa_s_kernel(tc, h1, W2, b2, W3, b3, out):
                 (nc.vector.tensor_copy, slice(0, TREES // 2)),
                 (nc.scalar.copy, slice(TREES // 2, TREES)),
             ):
-                copy(out=w3_grouped[:, trees], in_=w3_raw[:, trees].rearrange("p t j o -> p t o j"))
+                copy(
+                    out=w3_grouped[:, trees].rearrange("p t (c i) j -> p t c j i", i=PACK),
+                    in_=w3_raw[:, trees].rearrange("p t j (c i) -> p t c j i", i=PACK),
+                )
 
         def place_w3(t):
             return (t + t // (TREES // 2)) * D_OUT

@@ -28,6 +28,9 @@ VECTOR_COLUMNS = 60
 
 GROUPS = ((0, 1), (2, 3), (4, 5), (6,), (7,))
 
+IDLE_PASSES_FROM_TREE = 4
+IDLE_PASSES = 2
+
 LAYER1_LAG = 3
 
 FLOPS = 2 * TREES * BATCH * D_HID * D_MID + 2 * TREES * BATCH * D_MID * D_OUT
@@ -198,6 +201,18 @@ def tile_randomforestmlp_pa_s_kernel(tc, h1, W2, b2, W3, b3, out):
                     stop=True,
                 )
 
+        def keep_clock_up(t):
+            for n in range(IDLE_PASSES):
+                nc.tensor.matmul_mx(
+                    out=h1_psum[0][:].rearrange("p r u q -> p (r u q)"),
+                    lhsT=w2_words[t][:, 0:P].bitcast(FP8X4),
+                    lhsT_scale=w2_scales[t][:, 0:P],
+                    rhs=h1_words[:].bitcast(FP8X4),
+                    rhs_scale=h1_scales[:],
+                    start=True,
+                    stop=True,
+                )
+
         def add_bias(g):
             trees = GROUPS[g]
             nc.vector.tensor_tensor(
@@ -237,6 +252,8 @@ def tile_randomforestmlp_pa_s_kernel(tc, h1, W2, b2, W3, b3, out):
         for step in range(TREES + LAYER1_LAG + 2):
             if is_tree(step - LAYER1_LAG):
                 layer1(step - LAYER1_LAG)
+            if is_tree(step - LAYER1_LAG) and step - LAYER1_LAG >= IDLE_PASSES_FROM_TREE:
+                keep_clock_up(step - LAYER1_LAG)
             if is_tree(step):
                 regroup_w2(step)
             if step == TREES:

@@ -23,15 +23,15 @@ ROW_TILES = TREES * BATCH // P
 PAIR = 2
 BANK_TILES = 2
 
-VECTOR_COLUMNS_FIRST = 80
-VECTOR_COLUMNS = 60
+VECTOR_COLUMNS_FIRST = 72
+VECTOR_COLUMNS_DROP = 4
 
 GROUPS = ((0, 1), (2, 3), (4, 5), (6,), (7,))
 
-IDLE_PASSES_FROM_TREE = 4
+IDLE_PASSES_FROM_TREE = 0
 IDLE_PASSES = 2
 
-LAYER1_LAG = 3
+LAYER1_LAG = 2
 
 FLOPS = 2 * TREES * BATCH * D_HID * D_MID + 2 * TREES * BATCH * D_MID * D_OUT
 
@@ -61,7 +61,7 @@ def tile_randomforestmlp_pa_s_kernel(tc, h1, W2, b2, W3, b3, out):
         w3_grouped = grouped.tile([P, TREES, D_OUT, PACK], BF16, align_bytes=64)
         h1_grouped = grouped.tile([P, TREES * BATCH * PACK], BF16, align_bytes=64)
         h2_sum = [
-            per_tree.tile([P, len(g) * BATCH * PACK], F32 if len(g) > 1 else BF16, name="h2_sum") for g in GROUPS
+            per_tree.tile([P, len(g) * BATCH * PACK], BF16, name="h2_sum") for g in GROUPS
         ]
         h2_grouped = [
             per_tree.tile([P, len(g) * BATCH * PACK], BF16, align_bytes=64, name="h2_grouped") for g in GROUPS
@@ -143,7 +143,7 @@ def tile_randomforestmlp_pa_s_kernel(tc, h1, W2, b2, W3, b3, out):
             )
 
         def regroup_w2(t):
-            vector_columns = VECTOR_COLUMNS_FIRST if t == 0 else VECTOR_COLUMNS
+            vector_columns = VECTOR_COLUMNS_FIRST - t * VECTOR_COLUMNS_DROP
             for copy, columns in (
                 (nc.vector.tensor_copy, slice(0, vector_columns)),
                 (nc.scalar.copy, slice(vector_columns, P)),
@@ -161,11 +161,8 @@ def tile_randomforestmlp_pa_s_kernel(tc, h1, W2, b2, W3, b3, out):
             )
 
         def regroup_w3():
-            for copy, trees in (
-                (nc.vector.tensor_copy, slice(0, TREES // 2)),
-                (nc.scalar.copy, slice(TREES // 2, TREES)),
-            ):
-                copy(
+            for trees in (slice(0, TREES // 2), slice(TREES // 2, TREES)):
+                nc.scalar.copy(
                     out=w3_grouped[:, trees].rearrange("p t (c i) j -> p t c j i", i=PACK),
                     in_=w3_raw[:, trees].rearrange("p t j (c i) -> p t c j i", i=PACK),
                 )
@@ -223,10 +220,7 @@ def tile_randomforestmlp_pa_s_kernel(tc, h1, W2, b2, W3, b3, out):
             )
 
         def relu(g):
-            if len(GROUPS[g]) > 1:
-                nc.scalar.activation(out=h2_grouped[g][:], in_=h2_sum[g][:], func=mybir.ActivationFunctionType.Relu)
-            else:
-                nc.vector.tensor_scalar_max(out=h2_grouped[g][:], in0=h2_sum[g][:], scalar1=0.0)
+            nc.vector.tensor_scalar_max(out=h2_grouped[g][:], in0=h2_sum[g][:], scalar1=0.0)
 
         def place(t):
             return (t + [n for n in range(len(GROUPS)) if t in GROUPS[n]][0]) * BATCH
@@ -261,15 +255,15 @@ def tile_randomforestmlp_pa_s_kernel(tc, h1, W2, b2, W3, b3, out):
             if step == 0:
                 copy_h1(1, nc.scalar.copy)
                 quantise_h1(0)
-            if step == 2:
+            if step == 1:
                 prepare_biases()
             if is_tree(step - 1):
                 quantise_w2(step - 1)
             if step == 1:
                 quantise_h1(1)
-            if step == TREES:
-                quantise_w3(0)
             if step - 1 == TREES:
+                quantise_w3(0)
+            if step - 2 == TREES:
                 quantise_w3(1)
             for g in range(len(GROUPS)):
                 if bias_step(g) == step:

from contextlib import ExitStack

import concourse.mybir as mybir
from concourse.masks import make_identity

BF16 = mybir.dt.bfloat16
F32 = mybir.dt.float32
I32 = mybir.dt.int32
U32 = mybir.dt.uint32
U8 = mybir.dt.uint8
FP8X4 = mybir.dt.float8_e4m3fn_x4

P = 128
PACK = 4
TREES = 8
BATCH = 64
D_HID = 512
D_MID = 512
D_OUT = 64
assert D_HID == P * PACK and D_MID == P * PACK

ROW_TILES = TREES * BATCH // P
PAIR = 2
BANK_TILES = 2

VECTOR_COLUMNS_FIRST = 72
VECTOR_COLUMNS_DROP = 4

GROUPS = ((0, 1), (2, 3), (4, 5), (6,), (7,))

IDLE_PASSES_FROM_TREE = 0
IDLE_PASSES = 2

LAYER1_LAG = 2

FLOPS = 2 * TREES * BATCH * D_HID * D_MID + 2 * TREES * BATCH * D_MID * D_OUT


def tile_randomforestmlp_pa_s_kernel(tc, h1, W2, b2, W3, b3, out):
    nc = tc.nc
    with ExitStack() as ctx:
        const = ctx.enter_context(tc.tile_pool(name="const", bufs=1))
        raw = ctx.enter_context(tc.tile_pool(name="raw", bufs=1))
        grouped = ctx.enter_context(tc.tile_pool(name="grouped", bufs=1))
        packed = ctx.enter_context(tc.tile_pool(name="packed", bufs=1))
        per_tree = ctx.enter_context(tc.tile_pool(name="per_tree", bufs=TREES))
        psum_once = ctx.enter_context(tc.psum_pool(name="psum_once", bufs=1))
        psum_layer1 = ctx.enter_context(tc.psum_pool(name="psum_layer1", bufs=4))
        ctx.enter_context(tc.manual_schedule())

        w2_raw = [per_tree.tile([P, PACK, D_MID], BF16, name="w2_raw") for t in range(TREES)]
        w3_raw = raw.tile([P, TREES, PACK, D_OUT], BF16)
        h1_rows = raw.tile([P, ROW_TILES, D_HID], BF16)
        b2_columns = raw.tile([P, TREES, PACK], BF16)
        b2_rows = raw.tile([P, D_MID], BF16)
        b3_rows = raw.tile([P, D_OUT], BF16)

        w2_grouped = [
            per_tree.tile([P, PACK, P, PACK], BF16, align_bytes=64, name="w2_grouped") for t in range(TREES)
        ]
        w3_grouped = grouped.tile([P, TREES, D_OUT, PACK], BF16, align_bytes=64)
        h1_grouped = grouped.tile([P, TREES * BATCH * PACK], BF16, align_bytes=64)
        h2_sum = [
            per_tree.tile([P, len(g) * BATCH * PACK], BF16, name="h2_sum") for g in GROUPS
        ]
        h2_grouped = [
            per_tree.tile([P, len(g) * BATCH * PACK], BF16, align_bytes=64, name="h2_grouped") for g in GROUPS
        ]

        w2_words = [per_tree.tile([P, D_MID], U32, align_bytes=64, name="w2_words") for t in range(TREES)]
        w2_scales = [per_tree.tile([P, D_MID], U8, align_bytes=64, name="w2_scales") for t in range(TREES)]
        h1_words = packed.tile([P, TREES * BATCH], U32, align_bytes=64)
        h1_scales = packed.tile([P, TREES * BATCH], U8, align_bytes=64)
        h2_words = packed.tile([P, (TREES + len(GROUPS)) * BATCH], U32, align_bytes=64)
        h2_scales = packed.tile([P, (TREES + len(GROUPS)) * BATCH], U8, align_bytes=64)
        w3_words = packed.tile([P, (TREES + 2) * D_OUT], U32, align_bytes=64)
        w3_scales = packed.tile([P, (TREES + 2) * D_OUT], U8, align_bytes=64)

        identity = const.tile([P, P], F32)
        eighth = const.tile([P, P], BF16)
        table_warmer = const.tile([P, 1], BF16)
        b3_mean = const.tile([P, D_OUT], F32)
        out_rows = const.tile([BATCH, D_OUT], F32)

        def load_w2(t):
            nc.sync.dma_start(out=w2_raw[t][:], in_=W2[t].rearrange("(p j) n -> p j n", j=PACK))

        nc.vector.memset(b2_rows[:].bitcast(F32), 0.0)
        nc.vector.memset(b3_rows[:].bitcast(F32), 0.0)
        h1_tiles = h1.rearrange("t b k -> (t b) k").rearrange("(bank q r) k -> q bank r k", q=P, r=BANK_TILES)
        for bank in range(ROW_TILES // BANK_TILES):
            tiles = slice(bank * BANK_TILES, (bank + 1) * BANK_TILES)
            nc.sync.dma_start(out=h1_rows[:, tiles, :], in_=h1_tiles[:, bank])
        nc.sync.dma_start(out=b2_rows[0:TREES, :], in_=b2)
        nc.sync.dma_start(out=b3_rows[0:TREES, :], in_=b3)
        for t in range(TREES):
            load_w2(t)
        nc.sync.dma_start(out=w3_raw[:], in_=W3.rearrange("t (p j) o -> p t j o", j=PACK))

        make_identity(nc, identity[:])
        nc.vector.memset(eighth[:], 1.0 / TREES)
        nc.scalar.activation(out=table_warmer[:], in_=eighth[:, 0:1], func=mybir.ActivationFunctionType.Relu)
        nc.vector.memset(h2_words[:].bitcast(I32), 0)
        nc.vector.memset(h2_scales[:].bitcast(I32), 0)
        nc.vector.memset(w3_words[:].bitcast(I32), 0)
        nc.vector.memset(w3_scales[:].bitcast(I32), 0)

        def prepare_biases():
            bias_psum = psum_once.tile([P, PAIR * P + D_OUT], F32)
            b2_pairs = b2_rows[:].bitcast(F32).rearrange("t (c u) -> t u c", u=PAIR)
            for u in range(PAIR):
                nc.tensor.transpose(bias_psum[:, u * P : (u + 1) * P], b2_pairs[:, u, :], identity[:])
            nc.tensor.matmul(out=bias_psum[:, PAIR * P :], lhsT=eighth[:], rhs=b3_rows[:], start=True, stop=True)
            nc.scalar.copy(
                out=b2_columns[:].rearrange("c t i -> c (t i)").bitcast(F32).rearrange("c (t u) -> c t u", u=PAIR),
                in_=bias_psum[:, 0 : PAIR * P].rearrange("c (u t) -> c t u", u=PAIR)[:, 0:TREES, :],
            )
            nc.scalar.copy(out=b3_mean[:], in_=bias_psum[:, PAIR * P :])

        h1_pairs = h1_rows[:].rearrange("q r k -> q (r k)").bitcast(F32).rearrange("q (r p u) -> q r u p", r=ROW_TILES, u=PAIR)
        h1_grouped_pairs = h1_grouped[:].bitcast(F32).rearrange("p (bank q r u) -> p bank q r u", q=P, r=BANK_TILES, u=PAIR)
        h1_psum = {}

        def transpose_h1(bank):
            first = bank * BANK_TILES
            h1_psum[bank] = psum_once.tile([P, BANK_TILES, PAIR, P], F32, name="h1_psum%d" % bank)
            for r in range(BANK_TILES):
                for u in range(PAIR):
                    nc.tensor.transpose(h1_psum[bank][:, r, u, :], h1_pairs[:, first + r, u, :], identity[:])

        def copy_h1(bank, copy):
            copy(
                out=h1_grouped_pairs[:, bank],
                in_=h1_psum[bank][:].rearrange("p r u q -> p q r u"),
            )

        def quantise_h1(bank):
            rows = slice(bank * BANK_TILES * P, (bank + 1) * BANK_TILES * P)
            nc.vector.quantize_mx(
                out=h1_words[:, rows].bitcast(FP8X4),
                scales=h1_scales[:, rows],
                in_=h1_grouped[:, bank * BANK_TILES * P * PACK : (bank + 1) * BANK_TILES * P * PACK],
            )

        def regroup_w2(t):
            vector_columns = VECTOR_COLUMNS_FIRST - t * VECTOR_COLUMNS_DROP
            for copy, columns in (
                (nc.vector.tensor_copy, slice(0, vector_columns)),
                (nc.scalar.copy, slice(vector_columns, P)),
            ):
                copy(
                    out=w2_grouped[t][:, :, columns, :].rearrange("p i c j -> p c j i"),
                    in_=w2_raw[t][:].rearrange("p j (c i) -> p c j i", i=PACK)[:, columns],
                )

        def quantise_w2(t):
            nc.vector.quantize_mx(
                out=w2_words[t][:].bitcast(FP8X4),
                scales=w2_scales[t][:],
                in_=w2_grouped[t][:].rearrange("p i c j -> p (i c j)"),
            )

        def regroup_w3():
            for trees in (slice(0, TREES // 2), slice(TREES // 2, TREES)):
                nc.scalar.copy(
                    out=w3_grouped[:, trees].rearrange("p t (c i) j -> p t c j i", i=PACK),
                    in_=w3_raw[:, trees].rearrange("p t j (c i) -> p t c j i", i=PACK),
                )

        def place_w3(t):
            return (t + t // (TREES // 2)) * D_OUT

        def quantise_w3(half):
            first = half * (TREES // 2)
            columns = slice(place_w3(first), place_w3(first) + (TREES // 2) * D_OUT)
            nc.vector.quantize_mx(
                out=w3_words[:, columns].bitcast(FP8X4),
                scales=w3_scales[:, columns],
                in_=w3_grouped[:, first : first + TREES // 2].rearrange("p t o j -> p (t o j)"),
            )

        layer1_psum = {}

        def layer1(t):
            g = [n for n in range(len(GROUPS)) if t in GROUPS[n]][0]
            if t == GROUPS[g][0]:
                layer1_psum[g] = psum_layer1.tile([P, len(GROUPS[g]), PACK, BATCH], F32, name="layer1_psum")
            rows = slice(t * BATCH, (t + 1) * BATCH)
            for i in range(PACK):
                columns = slice(i * P, (i + 1) * P)
                nc.tensor.matmul_mx(
                    out=layer1_psum[g][:, t - GROUPS[g][0], i, :],
                    lhsT=w2_words[t][:, columns].bitcast(FP8X4),
                    lhsT_scale=w2_scales[t][:, columns],
                    rhs=h1_words[:, rows].bitcast(FP8X4),
                    rhs_scale=h1_scales[:, rows],
                    start=True,
                    stop=True,
                )

        def keep_clock_up(t):
            for n in range(IDLE_PASSES):
                nc.tensor.matmul_mx(
                    out=h1_psum[0][:].rearrange("p r u q -> p (r u q)"),
                    lhsT=w2_words[t][:, 0:P].bitcast(FP8X4),
                    lhsT_scale=w2_scales[t][:, 0:P],
                    rhs=h1_words[:].bitcast(FP8X4),
                    rhs_scale=h1_scales[:],
                    start=True,
                    stop=True,
                )

        def add_bias(g):
            trees = GROUPS[g]
            nc.vector.tensor_tensor(
                out=h2_sum[g][:].rearrange("p (t b i) -> p t b i", t=len(trees), i=PACK),
                in0=layer1_psum[g][:].rearrange("p t i b -> p t b i"),
                in1=b2_columns[:, trees[0] : trees[0] + len(trees)].unsqueeze(2).to_broadcast([P, len(trees), BATCH, PACK]),
                op=mybir.AluOpType.add,
            )

        def relu(g):
            nc.vector.tensor_scalar_max(out=h2_grouped[g][:], in0=h2_sum[g][:], scalar1=0.0)

        def place(t):
            return (t + [n for n in range(len(GROUPS)) if t in GROUPS[n]][0]) * BATCH

        def quantise_h2(g):
            rows = slice(place(GROUPS[g][0]), place(GROUPS[g][-1]) + BATCH)
            nc.vector.quantize_mx(
                out=h2_words[:, rows].bitcast(FP8X4),
                scales=h2_scales[:, rows],
                in_=h2_grouped[g][:],
            )

        for bank in range(ROW_TILES // BANK_TILES):
            transpose_h1(bank)
        copy_h1(0, nc.vector.tensor_copy)

        def is_tree(t):
            return 0 <= t < TREES

        def bias_step(g):
            return GROUPS[g][-1] + LAYER1_LAG

        for step in range(TREES + LAYER1_LAG + 2):
            if is_tree(step - LAYER1_LAG):
                layer1(step - LAYER1_LAG)
            if is_tree(step - LAYER1_LAG) and step - LAYER1_LAG >= IDLE_PASSES_FROM_TREE:
                keep_clock_up(step - LAYER1_LAG)
            if is_tree(step):
                regroup_w2(step)
            if step == TREES:
                regroup_w3()
            if step == 0:
                copy_h1(1, nc.scalar.copy)
                quantise_h1(0)
            if step == 1:
                prepare_biases()
            if is_tree(step - 1):
                quantise_w2(step - 1)
            if step == 1:
                quantise_h1(1)
            if step - 1 == TREES:
                quantise_w3(0)
            if step - 2 == TREES:
                quantise_w3(1)
            for g in range(len(GROUPS)):
                if bias_step(g) == step:
                    add_bias(g)
            for g in range(len(GROUPS)):
                if bias_step(g) + 1 == step:
                    relu(g)
            for g in range(len(GROUPS)):
                if bias_step(g) + 2 == step:
                    quantise_h2(g)

        layer2_psum = psum_once.tile([P, P], F32)
        for t in range(TREES):
            rows = slice(place(t), place(t) + P)
            columns = slice(place_w3(t), place_w3(t) + P)
            nc.tensor.matmul_mx(
                out=layer2_psum[:],
                lhsT=h2_words[:, rows].bitcast(FP8X4),
                lhsT_scale=h2_scales[:, rows],
                rhs=w3_words[:, columns].bitcast(FP8X4),
                rhs_scale=w3_scales[:, columns],
                start=(t == 0),
                stop=(t == TREES - 1),
            )
        nc.vector.scalar_tensor_tensor(
            out=out_rows[:],
            in0=layer2_psum[0:BATCH, 0:D_OUT],
            scalar=1.0 / TREES,
            in1=b3_mean[0:BATCH, :],
            op0=mybir.AluOpType.mult,
            op1=mybir.AluOpType.add,
        )
        nc.sync.dma_start(out=out, in_=out_rows[:])
